import numpy as np
import ml_dtypes


def mxq(x, axis, fmt="e4m3"):
    dtype, down = {"e4m3": (ml_dtypes.float8_e4m3fn, 7), "e5m2": (ml_dtypes.float8_e5m2, 14)}[fmt]
    v = np.moveaxis(np.asarray(x, np.float32).astype(ml_dtypes.bfloat16).astype(np.float64), axis, -1)
    blocks = v.reshape(v.shape[:-1] + (-1, 32))
    amax = np.abs(blocks).max(-1, keepdims=True)
    byte = np.maximum(np.where(amax > 0, np.frexp(amax)[1] - 1 + 127, 0) - down, 1)
    scale = np.exp2(byte - 127.0)
    codes = (blocks / scale).astype(np.float32).astype(dtype).astype(np.float64)
    return np.moveaxis((codes * scale).reshape(v.shape), -1, axis)


WIDE = False


def mx_kscale(k):
    if not WIDE:
        return np.ones(k)
    levels = np.array([18, -18])
    if k % 512:
        return np.exp2(np.random.permutation(np.resize(levels, k // 32))).repeat(32)
    a = np.empty((k // 512, 16))
    for p in range(k // 512):
        a[p, :8] = np.random.permutation(np.resize(levels, 8))
        for g in range(8):
            far = levels[np.abs(levels - a[p, g]) >= 10]
            a[p, g + 8] = far[np.random.randint(len(far))]
    return np.exp2(a.ravel()).repeat(32)


BF16 = ml_dtypes.bfloat16


def bf(x):
    return np.asarray(x, np.float32).astype(BF16)


def f64(x):
    return np.asarray(x).astype(np.float64)


B, T, C = 4, 256, 1024
EPS = 1e-8


def sigmoid(z):
    return 1.0 / (1.0 + np.exp(-z))


def shift_tokens(x, x_prev0):
    return np.concatenate([x_prev0[:, None, :], x[:, :-1, :]], axis=1)


def mix(x, xs, mu):
    return mu * x + (1.0 - mu) * xs


def setup_inputs():
    s = mx_kscale(B * T).reshape(B, T, 1)
    s_next = np.concatenate([s[:, 1:], s[:, -1:]], axis=1)
    sx = np.minimum(s, s_next)
    fu = mx_kscale(C)
    fv = mx_kscale(C)
    g = 1.0 / np.sqrt(C)
    x0 = bf(np.random.standard_normal((B, T, C)))
    a0 = bf(np.random.standard_normal((B, C)))
    b0 = bf(0.5 + np.random.uniform(size=(B, C)))
    p0 = bf(np.random.standard_normal((B, C)))
    w = bf((0.5 + 2.0 * np.random.uniform(size=C)) / T)
    u = bf(np.random.standard_normal(C) * 0.5)
    mu_r = bf(np.random.uniform(size=C))
    mu_k = bf(np.random.uniform(size=C))
    mu_v = bf(np.random.uniform(size=C))
    W_r = bf(np.random.standard_normal((C, C)) * g)
    W_k0 = bf(np.random.standard_normal((C, C)) * g)
    W_v = bf(np.random.standard_normal((C, C)) * g)
    W_out0 = bf(np.random.standard_normal((C, C)) * 2.0 * g)
    grad_out = bf(np.random.standard_normal((B, T, C)) * np.exp2(np.random.randint(-6, 1, (B, T, 1))) / s * fu)
    xf = f64(x0)
    xs = shift_tokens(xf, f64(p0))
    gate = sigmoid(mix(xf, xs, f64(mu_r)) @ f64(W_r).T)
    key = mix(xf, xs, f64(mu_k)) @ f64(W_k0).T
    value = mix(xf, xs, f64(mu_v)) @ f64(W_v).T
    return {
        "x": bf(f64(x0) * sx),
        "a0": a0,
        "b0": b0,
        "x_prev0": bf(f64(p0) * s[:, 0]),
        "w": w,
        "u": u,
        "mu_r": mu_r,
        "mu_k": mu_k,
        "mu_v": mu_v,
        "W_r": W_r,
        "W_k": bf(f64(W_k0) / fv[:, None]),
        "W_v": W_v,
        "W_out": bf(f64(W_out0) * fv[None, :] / fu[:, None]),
        "gate": np.asarray(gate, np.float32),
        "key": np.asarray(key, np.float32),
        "value": np.asarray(value, np.float32),
        "grad_out": grad_out,
    }


def reference(x, a0, b0, x_prev0, w, u, mu_r, mu_k, mu_v, W_r, W_k, W_v, W_out, gate, key, value, grad_out):
    n = B * T
    xf = f64(x)
    xs = shift_tokens(xf, f64(x_prev0))
    xk = mix(xf, xs, f64(mu_k)).reshape(n, C)
    diff = (xf - xs).reshape(n, C)
    rf, kf, vf = f64(gate), f64(key), f64(value)
    gq = mxq(f64(grad_out).reshape(n, C), 1, "e5m2")
    dh = gq @ mxq(f64(W_out), 0, "e4m3")
    ek = np.exp(f64(u) + kf)
    steps = 1.0 + np.arange(T)
    decay_pow = np.exp(-f64(w)[None, :] * steps[:, None])
    a_t = f64(a0)[:, None, :] * decay_pow[None]
    b_t = f64(b0)[:, None, :] * decay_pow[None]
    den = b_t + ek + EPS
    wkv = (a_t + ek * vf) / den
    dk = (dh.reshape(B, T, C) * rf * ek * (vf - wkv) / den).reshape(n, C)
    dxk = mxq(dk, 1, "e5m2") @ mxq(f64(W_k), 0, "e4m3")
    dmu_k = np.sum(dxk * diff, axis=0)
    dW_k = mxq(dk, 0, "e5m2").T @ mxq(xk, 0, "e4m3")
    return dmu_k, dW_k

@@ -1,0 +1,492 @@
+from contextlib import ExitStack
+
+import concourse.mybir as mybir
+from concourse.masks import make_identity
+
+F32 = mybir.dt.float32
+BF16 = mybir.dt.bfloat16
+U32 = mybir.dt.uint32
+U8 = mybir.dt.uint8
+E4M3 = mybir.dt.float8_e4m3fn_x4
+E5M2 = mybir.dt.float8_e5m2_x4
+ALU = mybir.AluOpType
+ACT = mybir.ActivationFunctionType
+
+B, T, C = 4, 256, 1024
+EPS = 1e-8
+FLOPS = 3 * 2 * (B * T) * C * C
+BYTES = 4 * 2 * 1024 * 1024 + 3 * 4 * 1024 * 1024 + 3 * 2 * B * C + 3 * 2 * C + 4 * 1024 * 1024 + 4 * C
+
+P = 128
+ROW_A0, ROW_B0, ROW_W, ROW_U, ROW_MU = 0, 32, 64, 72, 80
+
+
+def tile_rwkv_timemix_pa_v_kernel(
+    tc, x, a0, b0, x_prev0, w, u, mu_r, mu_k, mu_v, W_r, W_k, W_v, W_out, gate, key, value, grad_out, out_0, out_1
+):
+    nc = tc.nc
+    V, S, G, PE = nc.vector, nc.scalar, nc.gpsimd, nc.tensor
+
+    def tokens(ap):
+        return ap.rearrange("b (q j) c -> (b q) j c", j=4)
+
+    x_t, grad_t, key_t, val_t, gate_t = tokens(x), tokens(grad_out), tokens(key), tokens(value), tokens(gate)
+    wo_t = W_out.rearrange("(o p j) c -> o p j c", p=P, j=4)
+    wk_t = W_k.rearrange("(o p j) c -> o p j c", p=P, j=4)
+
+    with ExitStack() as ctx:
+        const = ctx.enter_context(tc.tile_pool(name="const", bufs=1))
+        st = ctx.enter_context(tc.tile_pool(name="st", bufs=2))
+        psum = ctx.enter_context(tc.psum_pool(name="psum", bufs=2))
+
+        def ctile(name, shape, dt):
+            return const.tile(shape, dt, name=name, tag=name, bufs=1, align_bytes=64)
+
+        def stile(tag, shape, dt, bufs):
+            return st.tile(shape, dt, name=tag, tag=tag, bufs=bufs, align_bytes=64)
+
+        def bank(tag, shape=(P, 512), dt=F32, bufs=3):
+            return psum.tile(list(shape), dt, name=tag, tag=tag, bufs=bufs)
+
+        ident = ctile("ident", [P, P], F32)
+        ident_b = ctile("ident_b", [P, P], BF16)
+        ones = ctile("ones", [P, P], F32)
+        steps = ctile("steps", [P, 256], F32)
+        vt = ctile("vt", [P, P], BF16)
+        vc = ctile("vc", [P, P], F32)
+        mut = ctile("mut", [P, 8], BF16)
+        eu = ctile("eu", [P, 8], F32)
+        negw = ctile("negw", [P, 8], F32)
+        beps = ctile("beps", [P, 8], F32)
+        b0u = ctile("b0u", [P, 32], F32)
+        b0m = ctile("b0m", [P, 32], F32)
+        rb = ctile("rb", [P, 32], F32)
+        c0 = ctile("c0", [P, 32], F32)
+        nc1 = ctile("nc1", [P, 32], F32)
+        dtab = ctile("dtab", [P, 8, 256], F32)
+        mub = ctile("mub", [P, C], F32)
+        dummy = ctile("dummy", [P, 1], F32)
+
+        wo_c = [ctile("wo_c%d" % o, [P, C], U32) for o in range(2)]
+        wo_s = [ctile("wo_s%d" % o, [P, C], U8) for o in range(2)]
+        wk_c = [ctile("wk_c%d" % o, [P, C], U32) for o in range(2)]
+        wk_s = [ctile("wk_s%d" % o, [P, C], U8) for o in range(2)]
+        gr_c = [ctile("gr_c%d" % g, [P, 2, 512], U32) for g in range(2)]
+        gr_s = [ctile("gr_s%d" % g, [P, 2, 512], U8) for g in range(2)]
+        xk_c = [ctile("xk_c%d" % g, [P, C], U32) for g in range(2)]
+        xk_s = [ctile("xk_s%d" % g, [P, C], U8) for g in range(2)]
+        dk_c = [[ctile("dk_c%d%d" % (g, h), [P, 512], U32) for h in range(2)] for g in range(2)]
+        dk_s = [[ctile("dk_s%d%d" % (g, h), [P, 512], U8) for h in range(2)] for g in range(2)]
+        dt_c, dt_s = {}, {}
+        for h in range(2):
+            dt_c[h] = ctile("dt_c%d" % h, [P, 512], U32)
+            dt_s[h] = ctile("dt_s%d" % h, [P, 512], U8)
+
+        V.memset(dummy[:], 0.0)
+        V.memset(vt[:], 0.0)
+        V.memset(ones[:], 1.0)
+        make_identity(nc, ident_b[:])
+        make_identity(nc, ident[:])
+        G.iota(steps[:].rearrange("p (j q) -> p j q", j=4), pattern=[[1, 4], [4, 64]], base=1, channel_multiplier=0,
+               allow_small_or_imprecise_dtypes=True)
+
+        with tc.manual_schedule():
+            S.activation(out=dummy[:], in_=dummy[:], func=ACT.Exp)
+            nc.sync.dma_start(out=vt[ROW_W : ROW_W + 8, :], in_=w.rearrange("(r p) -> r p", p=P))
+            nc.sync.dma_start(out=vt[ROW_U : ROW_U + 8, :], in_=u.rearrange("(r p) -> r p", p=P))
+            nc.sync.dma_start(out=vt[ROW_B0 : ROW_B0 + 32, :], in_=b0.rearrange("b (r p) -> (b r) p", p=P))
+            nc.sync.dma_start(out=vt[ROW_A0 : ROW_A0 + 32, :], in_=a0.rearrange("b (r p) -> (b r) p", p=P))
+            nc.sync.dma_start(out=vt[ROW_MU : ROW_MU + 8, :], in_=mu_k.rearrange("(r p) -> r p", p=P))
+
+            units = [(g, h, jp) for g in range(2) for h in range(2) for jp in range(2)]
+            key_s, val_s, gate_s, raw_s, xm_s = {}, {}, {}, {}, {}
+
+            def load_unit(store, tag, src, i, bufs):
+                g, h, jp = units[i]
+                t = stile(tag, [P, 2, 512], F32, bufs)
+                nc.sync.dma_start(
+                    out=t[:], in_=src[128 * g : 128 * g + 128, 2 * jp : 2 * jp + 2, 512 * h : 512 * h + 512]
+                )
+                store[i] = t
+
+            def load_key(i):
+                load_unit(key_s, "key", key_t, i, 4)
+
+            def load_val(i):
+                load_unit(val_s, "val", val_t, i, 3)
+
+            def load_gate(i):
+                load_unit(gate_s, "gate", gate_t, i, 2)
+
+            def load_raw(name, src):
+                t = stile("raw", [P, 4, C], BF16, 2)
+                nc.sync.dma_start(out=t[:], in_=src)
+                raw_s[name] = t
+
+            def load_x(g):
+                t = stile("xm", [P, 5, C], BF16, 1)
+                nc.sync.dma_start(out=t[:, 1:5, :], in_=x_t[128 * g : 128 * g + 128])
+                nc.sync.dma_start(out=t[1:64, 0, :], in_=x_t[128 * g : 128 * g + 63, 3, :])
+                nc.sync.dma_start(out=t[65:128, 0, :], in_=x_t[128 * g + 64 : 128 * g + 127, 3, :])
+                nc.sync.dma_start(out=t[0:1, 0, :], in_=x_prev0[2 * g : 2 * g + 1, :])
+                nc.sync.dma_start(out=t[64:65, 0, :], in_=x_prev0[2 * g + 1 : 2 * g + 2, :])
+                xm_s[g] = t
+
+            load_x(0)
+            load_key(0)
+            load_key(1)
+
+            vps = bank("tp", (P, P), BF16)
+            PE.transpose(vps[:], vt[:], ident_b[:])
+            V.tensor_copy(out=vc[:], in_=vps[:])
+            V.tensor_copy(out=mut[:], in_=vps[:, ROW_MU : ROW_MU + 8])
+            S.activation(out=eu[:], in_=vc[:, ROW_U : ROW_U + 8], func=ACT.Exp, scale=-1.0)
+            V.tensor_scalar(out=negw[:], in0=vc[:, ROW_W : ROW_W + 8], scalar1=-1.0, scalar2=None, op0=ALU.mult)
+            V.tensor_scalar(out=b0m[:], in0=vc[:, ROW_B0 : ROW_B0 + 32], scalar1=1e-30, scalar2=None, op0=ALU.max)
+            V.tensor_scalar(out=beps[:], in0=eu[:], scalar1=EPS, scalar2=None, op0=ALU.mult)
+
+            def per_b(t):
+                return t[:].rearrange("p (b r) -> p b r", b=4)
+
+            def over_b(t):
+                return t[:].unsqueeze(1).to_broadcast([P, 4, 8])
+
+            V.tensor_tensor(out=per_b(b0u), in0=vc[:, ROW_B0 : ROW_B0 + 32].rearrange("p (b r) -> p b r", b=4),
+                            in1=over_b(eu), op=ALU.mult)
+            V.reciprocal(out=rb[:], in_=b0m[:])
+            V.tensor_tensor(out=c0[:], in0=rb[:], in1=vc[:, ROW_A0 : ROW_A0 + 32], op=ALU.mult)
+            V.scalar_tensor_tensor(out=per_b(nc1), in0=per_b(c0), scalar=-1.0, in1=over_b(beps), op0=ALU.mult, op1=ALU.mult)
+
+            for r in range(8):
+                S.activation(out=dtab[:, r, :], in_=steps[:], func=ACT.Exp, scale=negw[:, r : r + 1])
+            for half in range(2):
+                mps = bank("dh")
+                for r in range(4):
+                    rr = 4 * half + r
+                    PE.matmul(mps[:, 128 * r : 128 * r + 128], lhsT=mut[:, rr : rr + 1].to_broadcast([P, P]), rhs=ident_b[:],
+                              start=True, stop=True)
+                V.tensor_copy(out=mub[:, 512 * half : 512 * half + 512], in_=mps[:])
+
+            tl, rt = {}, {}
+
+            def table_ln(Q):
+                g, h = Q
+                t = stile("tl", [P, 4, 512], F32, 2)
+                for r in range(4):
+                    ct = 4 * h + r
+                    dst = t[:, r, :].rearrange("p (j b q) -> p j b q", j=4, b=2)
+                    for b2 in range(2):
+                        col = 8 * (2 * g + b2) + ct
+                        S.activation(out=dst[:, :, b2, :], in_=dtab[:, ct, :].rearrange("p (j q) -> p j q", j=4), func=ACT.Ln,
+                                     scale=b0u[:, col : col + 1], bias=beps[:, ct : ct + 1])
+                tl[Q] = t
+
+            def table_exp(Q):
+                t = stile("rt", [P, 4, 512], F32, 2)
+                S.activation(out=t[:], in_=tl[Q][:], func=ACT.Exp, scale=-1.0)
+                rt[Q] = t
+
+            def table_ra(Q):
+                g, h = Q
+                for r in range(4):
+                    ct = 4 * h + r
+                    v = rt[Q][:, r, :].rearrange("p (j b q) -> p j b q", j=4, b=2)
+                    for b2 in range(2):
+                        col = 8 * (2 * g + b2) + ct
+                        G.tensor_scalar(out=v[:, :, b2, :], in0=v[:, :, b2, :], scalar1=nc1[:, col : col + 1],
+                                        scalar2=c0[:, col : col + 1], op0=ALU.mult, op1=ALU.add)
+
+            dh_s, dkq = {}, {}
+
+            def flip_table(tab, i, jj):
+                g, h, jp = units[i]
+                j = 2 * jp + jj
+                tp = bank("tp")
+                for r in range(4):
+                    PE.transpose(tp[:, 128 * r : 128 * r + 128], tab[(g, h)][:, r, 128 * j : 128 * j + 128], ident[:])
+                return tp
+
+            tp_s = {}
+
+            def pe_z(i, jj):
+                tp_s[("z", i, jj)] = flip_table(tl, i, jj)
+
+            def st_z(i, jj):
+                V.tensor_tensor(out=key_s[i][:, jj, :], in0=key_s[i][:, jj, :], in1=tp_s[("z", i, jj)][:], op=ALU.subtract)
+
+            def pe_q(i, jj):
+                tp_s[("q", i, jj)] = flip_table(rt, i, jj)
+
+            def st_s(i):
+                S.activation(out=key_s[i][:], in_=key_s[i][:], func=ACT.Sigmoid)
+
+            def st_q(i, jj):
+                V.tensor_tensor(out=val_s[i][:, jj, :], in0=tp_s[("q", i, jj)][:], in1=val_s[i][:, jj, :], op=ALU.subtract)
+
+            def st_y(i):
+                V.tensor_tensor(out=val_s[i][:], in0=val_s[i][:], in1=gate_s[i][:], op=ALU.mult)
+
+            def st_g(i):
+                k = key_s[i]
+                V.scalar_tensor_tensor(out=k[:], in0=k[:], scalar=1.0, in1=k[:], op0=ALU.subtract, op1=ALU.mult)
+
+            def st_p(i):
+                V.tensor_tensor(out=val_s[i][:], in0=val_s[i][:], in1=key_s[i][:], op=ALU.mult)
+
+            def st_dh(i, jj):
+                g, h, jp = units[i]
+                j = 2 * jp + jj
+                ps = bank("dh")
+                for o in range(2):
+                    PE.matmul_mx(ps[:], lhsT=gr_c[g][:, o, 128 * j : 128 * j + 128].bitcast(E5M2),
+                                 lhsT_scale=gr_s[g][:, o, 128 * j : 128 * j + 128],
+                                 rhs=wo_c[o][:, 512 * h : 512 * h + 512].bitcast(E4M3),
+                                 rhs_scale=wo_s[o][:, 512 * h : 512 * h + 512], start=(o == 0), stop=(o == 1))
+                dh_s[(i, jj)] = ps
+
+            def st_d(i, jj):
+                g, h, jp = units[i]
+                if (g, h) not in dkq:
+                    dkq[(g, h)] = stile("dkq", [P, 4, 512], BF16, 2)
+                V.tensor_tensor(out=dkq[(g, h)][:, 2 * jp + jj, :], in0=dh_s[(i, jj)][:], in1=val_s[i][:, jj, :], op=ALU.mult)
+
+            def words_view(til):
+                return til.bitcast(F32).rearrange("p (j r e) -> p j r e", r=128, e=2)
+
+            til_s = {}
+
+            def flip_words(src, j0, col0, out_til):
+                tp = bank("tp")
+                for jj in range(2):
+                    wds = src[:, j0 + jj, :].bitcast(F32)
+                    for e in range(2):
+                        k = 2 * jj + e
+                        PE.transpose(tp[:, 128 * k : 128 * k + 128], wds[:, col0 + e : col0 + 256 : 2], ident[:])
+                S.copy(out=words_view(out_til), in_=tp[:].rearrange("p (j e r) -> p j r e", j=2, e=2))
+
+            def grad_flip(g, o, jp):
+                if jp == 0:
+                    til_s[("g", g, o)] = stile("til", [P, 2048], BF16, 3)
+                flip_words(raw_s["g%d" % g], 2 * jp, 256 * o, til_s[("g", g, o)][:, 1024 * jp : 1024 * jp + 1024])
+
+            def grad_quant(g, o):
+                if True:
+                    V.quantize_mx(out=gr_c[g][:, o, :].bitcast(E5M2), scales=gr_s[g][:, o, :], in_=til_s[("g", g, o)][:])
+
+            def il_view(t):
+                return t.rearrange("p (a i t) -> p a t i", i=4, t=4)
+
+            def src_view(ap):
+                return ap.rearrange("p t (a i) -> p a t i", i=4)
+
+            il_s = {}
+
+            def w_il(name, half, eng):
+                t = stile("il", [P, 2048], BF16, 3)
+                src = src_view(raw_s[name][:, :, 512 * half : 512 * half + 512])
+                if eng is V:
+                    V.tensor_copy(out=il_view(t[:]), in_=src)
+                elif eng is G:
+                    G.tensor_scalar(out=il_view(t[:]), in0=src, scalar1=1.0, scalar2=0.0, op0=ALU.mult, op1=ALU.add)
+                else:
+                    S.copy(out=il_view(t[:]), in_=src)
+                il_s[(name, half)] = t
+
+            def w_quant(name, half, codes, scales):
+                sl = slice(512 * half, 512 * half + 512)
+                V.quantize_mx(out=codes[:, sl].bitcast(E4M3), scales=scales[:, sl], in_=il_s[(name, half)][:])
+
+            diff_s, m_s = {}, {}
+
+            def x_diff(g, nh, eng=G):
+                t = stile("diff", [P, 4, 512], F32, 3)
+                cs = slice(512 * nh, 512 * nh + 512)
+                eng.tensor_tensor(out=t[:], in0=xm_s[g][:, 1:5, cs], in1=xm_s[g][:, 0:4, cs], op=ALU.subtract)
+                diff_s[(g, nh)] = t
+
+            def x_mix(g, nh):
+                t = stile("il", [P, 2048], BF16, 3)
+                ms = []
+                for cc in range(2):
+                    m = stile("m", [P, 4, 256], F32, 2)
+                    col = 512 * nh + 256 * cc
+                    V.tensor_tensor(out=m[:], in0=diff_s[(g, nh)][:, :, 256 * cc : 256 * cc + 256],
+                                    in1=mub[:, col : col + 256].unsqueeze(1).to_broadcast([P, 4, 256]), op=ALU.mult)
+                    ms.append(m)
+                for cc in range(2):
+                    col = 512 * nh + 256 * cc
+                    V.tensor_tensor(out=il_view(t[:, 1024 * cc : 1024 * cc + 1024]), in0=src_view(ms[cc][:]),
+                                    in1=src_view(xm_s[g][:, 0:4, col : col + 256]), op=ALU.add)
+                il_s[("x", g, nh)] = t
+
+            def x_quant(g, nh):
+                sl = slice(512 * nh, 512 * nh + 512)
+                V.quantize_mx(out=xk_c[g][:, sl].bitcast(E4M3), scales=xk_s[g][:, sl], in_=il_s[("x", g, nh)][:])
+
+            def dkt_flip(i):
+                g, h, jp = units[i]
+                t = stile("til", [P, 2048], BF16, 3)
+                flip_words(dkq[(g, h)], 2 * jp, 0, t[:, 0:1024])
+                til_s[("d", i)] = t
+
+            def dkt_quant(i):
+                g, h, jp = units[i]
+                sl = slice(256 * jp, 256 * jp + 256)
+                V.quantize_mx(out=dt_c[h][:, sl].bitcast(E5M2), scales=dt_s[h][:, sl], in_=til_s[("d", i)][:, 0:1024])
+
+            def dk_il(Q, eng):
+                t = stile("il", [P, 2048], BF16, 3)
+                if eng is V:
+                    V.tensor_copy(out=il_view(t[:]), in_=src_view(dkq[Q][:]))
+                else:
+                    S.copy(out=il_view(t[:]), in_=src_view(dkq[Q][:]))
+                il_s[("d", Q)] = t
+
+            def dk_quant(Q):
+                g, h = Q
+                V.quantize_mx(out=dk_c[g][h][:].bitcast(E5M2), scales=dk_s[g][h][:], in_=il_s[("d", Q)][:])
+
+            sums = [bank("sum%d" % nh, bufs=1) for nh in range(2)]
+            pending = []
+            count = [0, 0]
+
+            def flush():
+                if pending:
+                    nh, prod = pending.pop(0)
+                    PE.matmul(sums[nh][:], lhsT=ones[:], rhs=prod[:], start=(count[nh] == 0), stop=(count[nh] == 7))
+                    count[nh] = count[nh] + 1
+
+            dx_s = {}
+
+            def pe_dx(g, j, nh):
+                ps = bank("dh")
+                for h in range(2):
+                    PE.matmul_mx(ps[:], lhsT=dt_c[h][:, 128 * j : 128 * j + 128].bitcast(E5M2),
+                                 lhsT_scale=dt_s[h][:, 128 * j : 128 * j + 128],
+                                 rhs=wk_c[h][:, 512 * nh : 512 * nh + 512].bitcast(E4M3),
+                                 rhs_scale=wk_s[h][:, 512 * nh : 512 * nh + 512], start=(h == 0), stop=(h == 1))
+                dx_s[(g, j, nh)] = ps
+
+            def st_dx(g, j, nh):
+                prod = stile("prod", [P, 512], F32, 4)
+                V.tensor_tensor(out=prod[:], in0=dx_s[(g, j, nh)][:], in1=diff_s[(g, nh)][:, j, :], op=ALU.mult)
+                pending.append((nh, prod))
+
+            def dw(h, co, engs, tag="dh"):
+                t = stile("key", [P, 2, 512], F32, 4)
+                for ci in range(2):
+                    ps = bank(tag)
+                    for g in range(2):
+                        PE.matmul_mx(ps[:], lhsT=dk_c[g][h][:, 128 * co : 128 * co + 128].bitcast(E5M2),
+                                     lhsT_scale=dk_s[g][h][:, 128 * co : 128 * co + 128],
+                                     rhs=xk_c[g][:, 512 * ci : 512 * ci + 512].bitcast(E4M3),
+                                     rhs_scale=xk_s[g][:, 512 * ci : 512 * ci + 512], start=(g == 0), stop=(g == 1))
+                    if engs[ci] is V:
+                        V.tensor_copy(out=t[:, ci, :], in_=ps[:])
+                    else:
+                        S.copy(out=t[:, ci, :], in_=ps[:])
+                r0 = 512 * h + 128 * co
+                nc.sync.dma_start(out=out_1[r0 : r0 + 128, :].rearrange("p (i c) -> p i c", i=2), in_=t[:])
+
+            made = set()
+
+            def F(f, *a):
+                def go():
+                    f(*a)
+                    made.add((f,) + tuple(v for v in a[:2] if isinstance(v, (int, str, tuple))))
+
+                return (None, go, ())
+
+            def Z(i, jj):
+                return (lambda: pe_z(i, jj), lambda: st_z(i, jj), ())
+
+            def Q(i, jj):
+                return (lambda: pe_q(i, jj), lambda: st_q(i, jj), ((table_ra, units[i][:2]),))
+
+            def D(i, jj):
+                return (lambda: st_dh(i, jj), lambda: st_d(i, jj), ((grad_quant, units[i][0], 1), (w_quant, "wo1", 1)))
+
+            def X(g, j, nh):
+                return (lambda: pe_dx(g, j, nh), lambda: st_dx(g, j, nh), ((dkt_quant, 4 * g + 2 + j // 2), (w_quant, "wk1", 1)))
+
+            def run(items, ahead):
+                front = 0
+                for k in range(-ahead, len(items)):
+                    while front < min(k + ahead + 1, len(items)) and all(t in made for t in items[front][2]):
+                        if items[front][0] is not None:
+                            items[front][0]()
+                        front += 1
+                    if k >= 0:
+                        assert front > k
+                        items[k][1]()
+
+            load_raw("wo0", wo_t[0])
+            load_key(2)
+            load_raw("wo1", wo_t[1])
+            load_val(0)
+            load_gate(0)
+            load_raw("g0", grad_t[0:128])
+            load_key(3)
+            load_val(1)
+            load_gate(1)
+            table_ln((0, 0))
+            table_ln((0, 1))
+            table_exp((0, 0))
+            table_exp((0, 1))
+
+            items = [
+                F(x_diff, 0, 1), F(x_diff, 0, 0, V), F(x_mix, 0, 0), F(w_il, "wo0", 0, G), Z(0, 0), Z(0, 1), F(x_quant, 0, 0),
+                F(st_s, 0), F(x_mix, 0, 1), F(w_il, "wo0", 1, G), F(table_ra, (0, 0)), F(table_ra, (0, 1)),
+                Z(1, 0), Z(1, 1), F(st_s, 1), F(x_quant, 0, 1), F(w_quant, "wo0", 0, wo_c[0], wo_s[0]), F(w_il, "wo1", 0, S),
+                Z(2, 0), Z(2, 1), F(w_il, "wo1", 1, S), F(w_quant, "wo0", 1, wo_c[0], wo_s[0]), Z(3, 0), Z(3, 1),
+                F(load_val, 2), F(load_raw, "wk0", wk_t[0]), F(load_x, 1), F(load_gate, 2),
+                Q(0, 0), F(st_g, 0), Q(0, 1), F(grad_flip, 0, 0, 0), F(st_y, 0), F(grad_flip, 0, 0, 1), Q(1, 0), F(st_p, 0),
+                F(grad_flip, 0, 1, 0), F(w_quant, "wo1", 0, wo_c[1], wo_s[1]), F(grad_flip, 0, 1, 1), F(st_s, 2), F(st_s, 3),
+                F(table_ln, (1, 0)), F(table_ln, (1, 1)), F(table_exp, (1, 0)), F(table_exp, (1, 1)), F(load_raw, "wk1", wk_t[1]),
+                F(st_g, 1), F(grad_quant, 0, 0), F(w_quant, "wo1", 1, wo_c[1], wo_s[1]), Q(1, 1), F(load_key, 4),
+                F(grad_quant, 0, 1), F(st_y, 1), F(st_p, 1),
+            ]
+            extra = {
+                0: [F(w_il, "wk0", 0, G), F(w_il, "wk0", 1, G), F(x_diff, 1, 0), F(table_ra, (1, 0)), F(table_ra, (1, 1))],
+                1: [F(w_quant, "wk0", 0, wk_c[0], wk_s[0]), F(load_raw, "g1", grad_t[128:256]), F(w_quant, "wk0", 1, wk_c[0], wk_s[0])],
+                2: [F(x_mix, 1, 0), F(grad_flip, 1, 0, 0), F(dkt_flip, 0), F(grad_flip, 1, 0, 1), F(dk_il, (0, 0), S), F(grad_flip, 1, 1, 0),
+                    F(x_quant, 1, 0), F(grad_flip, 1, 1, 1), F(dkt_quant, 0), F(w_il, "wk1", 0, S)],
+                3: [F(dkt_flip, 1), F(grad_quant, 1, 0), F(dk_quant, (0, 0)), F(grad_quant, 1, 1), F(dkt_flip, 2), F(w_quant, "wk1", 0, wk_c[1], wk_s[1]),
+                    F(w_il, "wk1", 1, S), F(dkt_quant, 1), F(dkt_quant, 2), F(dkt_flip, 3)],
+                4: [F(w_quant, "wk1", 1, wk_c[1], wk_s[1]), F(dk_il, (0, 1), S), X(0, 0, 0), X(0, 0, 1), F(dkt_quant, 3), F(flush), X(0, 1, 0), F(flush), X(0, 1, 1), F(flush),
+                    F(dk_quant, (0, 1)), F(flush), F(dkt_flip, 4)],
+                5: [X(0, 2, 0), X(0, 2, 1), F(flush), F(dkt_quant, 4), X(0, 3, 0), F(flush), F(dkt_flip, 5), X(0, 3, 1), F(x_diff, 1, 1), F(flush),
+                    F(flush), F(dk_il, (1, 0), S), F(dkt_quant, 5)],
+                6: [F(x_mix, 1, 1), F(dk_quant, (1, 0)), F(dkt_flip, 6), F(x_quant, 1, 1), F(dw, 0, 0, (S, S)), F(dkt_quant, 6), F(dw, 0, 1, (S, S)), X(1, 0, 0), X(1, 0, 1), F(dw, 0, 2, (S, S)), F(flush), F(flush)],
+                7: [F(dkt_flip, 7), F(dk_il, (1, 1), V), X(1, 1, 0), F(dk_quant, (1, 1)), X(1, 1, 1), F(dkt_quant, 7), F(flush), F(flush), X(1, 2, 0), X(1, 2, 1), X(1, 3, 0), X(1, 3, 1),
+                    F(dw, 0, 3, (S, S)), F(dw, 1, 0, (S, V)), F(dw, 1, 1, (S, V)), F(flush), F(dw, 1, 2, (S, V)), F(flush), F(dw, 1, 3, (S, V)),
+                     F(flush), F(flush)],
+            }
+            for i in range(8):
+                base = [D(i, 0), D(i, 1)]
+                if 1 <= i < 7:
+                    base = [Q(i + 1, 0), D(i, 0), Q(i + 1, 1), D(i, 1), F(st_g, i + 1), F(st_y, i + 1), F(st_p, i + 1)]
+                if i == 0:
+                    base = [D(0, 0), D(0, 1)]
+                if 1 <= i <= 4:
+                    base += [Z(i + 3, 0), Z(i + 3, 1), F(st_s, i + 3)]
+                if i + 5 < 8:
+                    base.append(F(load_key, i + 5))
+                if i + 3 < 8:
+                    base += [F(load_gate, i + 3), F(load_val, i + 3)]
+                ex = extra[i]
+                lead = 4 if 1 <= i < 7 else len(base)
+                items += base[:lead]
+                rest = base[lead:]
+                while rest or ex:
+                    if rest:
+                        items.append(rest[0])
+                        rest = rest[1:]
+                    if ex:
+                        items.append(ex[0])
+                        ex = ex[1:]
+            run(items, 3)
+            row = stile("gate", [P, 2, 512], F32, 2)
+            S.copy(out=row[0:1, 0, :], in_=sums[0][0:1, :])
+            S.copy(out=row[0:1, 1, :], in_=sums[1][0:1, :])
+            nc.sync.dma_start(out=out_0.rearrange("(o i c) -> o i c", o=1, i=2), in_=row[0:1, :, :])

@@ -45,16 +45,16 @@ def tile_rwkv_timemix_pa_v_kernel(
         def stile(tag, shape, dt, bufs):
             return st.tile(shape, dt, name=tag, tag=tag, bufs=bufs, align_bytes=64)
 
-        def bank(tag, shape=(P, 512), dt=F32, bufs=3):
-            return psum.tile(list(shape), dt, name=tag, tag=tag, bufs=bufs)
+        banks = {"tp": 3, "dh": 3, "xp": 2}
+
+        def bank(tag, shape=(P, 512), dt=F32):
+            return psum.tile(list(shape), dt, name=tag, tag=tag, bufs=banks[tag])
 
         ident = ctile("ident", [P, P], F32)
         ident_b = ctile("ident_b", [P, P], BF16)
-        ones = ctile("ones", [P, P], F32)
         steps = ctile("steps", [P, 256], F32)
         vt = ctile("vt", [P, P], BF16)
         vc = ctile("vc", [P, P], F32)
-        mut = ctile("mut", [P, 8], BF16)
         eu = ctile("eu", [P, 8], F32)
         negw = ctile("negw", [P, 8], F32)
         beps = ctile("beps", [P, 8], F32)
@@ -64,7 +64,8 @@ def tile_rwkv_timemix_pa_v_kernel(
         c0 = ctile("c0", [P, 32], F32)
         nc1 = ctile("nc1", [P, 32], F32)
         dtab = ctile("dtab", [P, 8, 256], F32)
-        mub = ctile("mub", [P, C], F32)
+        acc = ctile("acc", [P, 16], F32)
+        tot = ctile("tot", [P, P], F32)
         dummy = ctile("dummy", [P, 1], F32)
 
         wo_c = [ctile("wo_c%d" % o, [P, C], U32) for o in range(2)]
@@ -84,7 +85,7 @@ def tile_rwkv_timemix_pa_v_kernel(
 
         V.memset(dummy[:], 0.0)
         V.memset(vt[:], 0.0)
-        V.memset(ones[:], 1.0)
+        G.memset(tot[:], 0.0)
         make_identity(nc, ident_b[:])
         make_identity(nc, ident[:])
         G.iota(steps[:].rearrange("p (j q) -> p j q", j=4), pattern=[[1, 4], [4, 64]], base=1, channel_multiplier=0,
@@ -139,7 +140,6 @@ def tile_rwkv_timemix_pa_v_kernel(
             vps = bank("tp", (P, P), BF16)
             PE.transpose(vps[:], vt[:], ident_b[:])
             V.tensor_copy(out=vc[:], in_=vps[:])
-            V.tensor_copy(out=mut[:], in_=vps[:, ROW_MU : ROW_MU + 8])
             S.activation(out=eu[:], in_=vc[:, ROW_U : ROW_U + 8], func=ACT.Exp, scale=-1.0)
             V.tensor_scalar(out=negw[:], in0=vc[:, ROW_W : ROW_W + 8], scalar1=-1.0, scalar2=None, op0=ALU.mult)
             V.tensor_scalar(out=b0m[:], in0=vc[:, ROW_B0 : ROW_B0 + 32], scalar1=1e-30, scalar2=None, op0=ALU.max)
@@ -159,13 +159,6 @@ def tile_rwkv_timemix_pa_v_kernel(
 
             for r in range(8):
                 S.activation(out=dtab[:, r, :], in_=steps[:], func=ACT.Exp, scale=negw[:, r : r + 1])
-            for half in range(2):
-                mps = bank("dh")
-                for r in range(4):
-                    rr = 4 * half + r
-                    PE.matmul(mps[:, 128 * r : 128 * r + 128], lhsT=mut[:, rr : rr + 1].to_broadcast([P, P]), rhs=ident_b[:],
-                              start=True, stop=True)
-                V.tensor_copy(out=mub[:, 512 * half : 512 * half + 512], in_=mps[:])
 
             tl, rt = {}, {}
 
@@ -193,8 +186,8 @@ def tile_rwkv_timemix_pa_v_kernel(
                     v = rt[Q][:, r, :].rearrange("p (j b q) -> p j b q", j=4, b=2)
                     for b2 in range(2):
                         col = 8 * (2 * g + b2) + ct
-                        G.tensor_scalar(out=v[:, :, b2, :], in0=v[:, :, b2, :], scalar1=nc1[:, col : col + 1],
-                                        scalar2=c0[:, col : col + 1], op0=ALU.mult, op1=ALU.add)
+                        S.activation(out=v[:, :, b2, :], in_=v[:, :, b2, :], func=ACT.Identity, scale=nc1[:, col : col + 1],
+                                     bias=c0[:, col : col + 1])
 
             dh_s, dkq = {}, {}
 
@@ -266,7 +259,7 @@ def tile_rwkv_timemix_pa_v_kernel(
 
             def grad_flip(g, o, jp):
                 if jp == 0:
-                    til_s[("g", g, o)] = stile("til", [P, 2048], BF16, 3)
+                    til_s[("g", g, o)] = stile("til", [P, 2048], BF16, 2)
                 flip_words(raw_s["g%d" % g], 2 * jp, 256 * o, til_s[("g", g, o)][:, 1024 * jp : 1024 * jp + 1024])
 
             def grad_quant(g, o):
@@ -282,7 +275,7 @@ def tile_rwkv_timemix_pa_v_kernel(
             il_s = {}
 
             def w_il(name, half, eng):
-                t = stile("il", [P, 2048], BF16, 3)
+                t = stile("il", [P, 2048], BF16, 4)
                 src = src_view(raw_s[name][:, :, 512 * half : 512 * half + 512])
                 if eng is V:
                     V.tensor_copy(out=il_view(t[:]), in_=src)
@@ -296,28 +289,39 @@ def tile_rwkv_timemix_pa_v_kernel(
                 sl = slice(512 * half, 512 * half + 512)
                 V.quantize_mx(out=codes[:, sl].bitcast(E4M3), scales=scales[:, sl], in_=il_s[(name, half)][:])
 
-            diff_s, m_s = {}, {}
+            xt_s, df_s, xk_s2 = {}, {}, {}
 
-            def x_diff(g, nh, eng=G):
-                t = stile("diff", [P, 4, 512], F32, 3)
-                cs = slice(512 * nh, 512 * nh + 512)
-                eng.tensor_tensor(out=t[:], in0=xm_s[g][:, 1:5, cs], in1=xm_s[g][:, 0:4, cs], op=ALU.subtract)
-                diff_s[(g, nh)] = t
+            def x_flip(g, r, eng):
+                ps = bank("xp", (P, 640), BF16)
+                for s in range(5):
+                    PE.transpose(ps[:, 128 * s : 128 * s + 128], xm_s[g][:, s, 128 * r : 128 * r + 128], ident_b[:])
+                t = stile("xt", [P, 640], BF16, 3)
+                if eng is V:
+                    V.tensor_copy(out=t[:], in_=ps[:])
+                else:
+                    S.copy(out=t[:], in_=ps[:])
+                xt_s[(g, r)] = t
 
-            def x_mix(g, nh):
-                t = stile("il", [P, 2048], BF16, 3)
-                ms = []
-                for cc in range(2):
-                    m = stile("m", [P, 4, 256], F32, 2)
-                    col = 512 * nh + 256 * cc
-                    V.tensor_tensor(out=m[:], in0=diff_s[(g, nh)][:, :, 256 * cc : 256 * cc + 256],
-                                    in1=mub[:, col : col + 256].unsqueeze(1).to_broadcast([P, 4, 256]), op=ALU.mult)
-                    ms.append(m)
-                for cc in range(2):
-                    col = 512 * nh + 256 * cc
-                    V.tensor_tensor(out=il_view(t[:, 1024 * cc : 1024 * cc + 1024]), in0=src_view(ms[cc][:]),
-                                    in1=src_view(xm_s[g][:, 0:4, col : col + 256]), op=ALU.add)
-                il_s[("x", g, nh)] = t
+            def x_diff(g, r):
+                t = stile("df", [P, 512], F32, 14)
+                V.tensor_tensor(out=t[:], in0=xt_s[(g, r)][:, 128:640], in1=xt_s[(g, r)][:, 0:512], op=ALU.subtract)
+                df_s[(g, r)] = t
+
+            def x_mix(g, r):
+                t = stile("xk", [P, 512], BF16, 8)
+                V.scalar_tensor_tensor(out=t[:], in0=df_s[(g, r)][:], scalar=vc[:, ROW_MU + r : ROW_MU + r + 1],
+                                       in1=xt_s[(g, r)][:, 0:512], op0=ALU.mult, op1=ALU.add)
+                xk_s2[(g, r)] = t
+
+            def x_back(g, r, eng=None):
+                ps = bank("xp", (P, 512), BF16)
+                for j in range(4):
+                    PE.transpose(ps[:, 128 * j : 128 * j + 128], xk_s2[(g, r)][:, 128 * j : 128 * j + 128], ident_b[:])
+                if r % 4 == 0:
+                    il_s[("x", g, r // 4)] = stile("il", [P, 2048], BF16, 4)
+                k = r % 4
+                dst = il_s[("x", g, r // 4)][:, 512 * k : 512 * k + 512].rearrange("p (c t) -> p c t", t=4)
+                S.copy(out=dst, in_=ps[:].rearrange("p (t c) -> p c t", t=4))
 
             def x_quant(g, nh):
                 sl = slice(512 * nh, 512 * nh + 512)
@@ -325,7 +329,7 @@ def tile_rwkv_timemix_pa_v_kernel(
 
             def dkt_flip(i):
                 g, h, jp = units[i]
-                t = stile("til", [P, 2048], BF16, 3)
+                t = stile("til", [P, 2048], BF16, 2)
                 flip_words(dkq[(g, h)], 2 * jp, 0, t[:, 0:1024])
                 til_s[("d", i)] = t
 
@@ -335,7 +339,7 @@ def tile_rwkv_timemix_pa_v_kernel(
                 V.quantize_mx(out=dt_c[h][:, sl].bitcast(E5M2), scales=dt_s[h][:, sl], in_=til_s[("d", i)][:, 0:1024])
 
             def dk_il(Q, eng):
-                t = stile("il", [P, 2048], BF16, 3)
+                t = stile("il", [P, 2048], BF16, 4)
                 if eng is V:
                     V.tensor_copy(out=il_view(t[:]), in_=src_view(dkq[Q][:]))
                 else:
@@ -346,33 +350,22 @@ def tile_rwkv_timemix_pa_v_kernel(
                 g, h = Q
                 V.quantize_mx(out=dk_c[g][h][:].bitcast(E5M2), scales=dk_s[g][h][:], in_=il_s[("d", Q)][:])
 
-            sums = [bank("sum%d" % nh, bufs=1) for nh in range(2)]
-            pending = []
-            count = [0, 0]
-
-            def flush():
-                if pending:
-                    nh, prod = pending.pop(0)
-                    PE.matmul(sums[nh][:], lhsT=ones[:], rhs=prod[:], start=(count[nh] == 0), stop=(count[nh] == 7))
-                    count[nh] = count[nh] + 1
-
             dx_s = {}
 
-            def pe_dx(g, j, nh):
+            def pe_dx(g, r):
                 ps = bank("dh")
                 for h in range(2):
-                    PE.matmul_mx(ps[:], lhsT=dt_c[h][:, 128 * j : 128 * j + 128].bitcast(E5M2),
-                                 lhsT_scale=dt_s[h][:, 128 * j : 128 * j + 128],
-                                 rhs=wk_c[h][:, 512 * nh : 512 * nh + 512].bitcast(E4M3),
-                                 rhs_scale=wk_s[h][:, 512 * nh : 512 * nh + 512], start=(h == 0), stop=(h == 1))
-                dx_s[(g, j, nh)] = ps
+                    PE.matmul_mx(ps[:], lhsT=wk_c[h][:, 128 * r : 128 * r + 128].bitcast(E4M3),
+                                 lhsT_scale=wk_s[h][:, 128 * r : 128 * r + 128],
+                                 rhs=dt_c[h][:].bitcast(E5M2), rhs_scale=dt_s[h][:], start=(h == 0), stop=(h == 1))
+                dx_s[(g, r)] = ps
 
-            def st_dx(g, j, nh):
-                prod = stile("prod", [P, 512], F32, 4)
-                V.tensor_tensor(out=prod[:], in0=dx_s[(g, j, nh)][:], in1=diff_s[(g, nh)][:, j, :], op=ALU.mult)
-                pending.append((nh, prod))
+            def st_dx(g, r):
+                prod = stile("prod", [P, 512], F32, 1)
+                V.scalar_tensor_tensor(out=prod[:], in0=dx_s[(g, r)][:], scalar=1.0, in1=df_s[(g, r)][:], op0=ALU.mult, op1=ALU.mult,
+                                       accum_out=acc[:, 8 * g + r : 8 * g + r + 1])
 
-            def dw(h, co, engs, tag="dh"):
+            def dw(h, co, engs, tag="tp"):
                 t = stile("key", [P, 2, 512], F32, 4)
                 for ci in range(2):
                     ps = bank(tag)
@@ -406,8 +399,8 @@ def tile_rwkv_timemix_pa_v_kernel(
             def D(i, jj):
                 return (lambda: st_dh(i, jj), lambda: st_d(i, jj), ((grad_quant, units[i][0], 1), (w_quant, "wo1", 1)))
 
-            def X(g, j, nh):
-                return (lambda: pe_dx(g, j, nh), lambda: st_dx(g, j, nh), ((dkt_quant, 4 * g + 2 + j // 2), (w_quant, "wk1", 1)))
+            def X(g, r):
+                return (lambda: pe_dx(g, r), lambda: st_dx(g, r), ((dkt_quant, 4 * g + 2), (dkt_quant, 4 * g + 3), (w_quant, "wk1", 1)))
 
             def run(items, ahead):
                 front = 0
@@ -431,36 +424,35 @@ def tile_rwkv_timemix_pa_v_kernel(
             load_gate(1)
             table_ln((0, 0))
             table_ln((0, 1))
-            table_exp((0, 0))
-            table_exp((0, 1))
 
             items = [
-                F(x_diff, 0, 1), F(x_diff, 0, 0, V), F(x_mix, 0, 0), F(w_il, "wo0", 0, G), Z(0, 0), Z(0, 1), F(x_quant, 0, 0),
-                F(st_s, 0), F(x_mix, 0, 1), F(w_il, "wo0", 1, G), F(table_ra, (0, 0)), F(table_ra, (0, 1)),
-                Z(1, 0), Z(1, 1), F(st_s, 1), F(x_quant, 0, 1), F(w_quant, "wo0", 0, wo_c[0], wo_s[0]), F(w_il, "wo1", 0, S),
-                Z(2, 0), Z(2, 1), F(w_il, "wo1", 1, S), F(w_quant, "wo0", 1, wo_c[0], wo_s[0]), Z(3, 0), Z(3, 1),
-                F(load_val, 2), F(load_raw, "wk0", wk_t[0]), F(load_x, 1), F(load_gate, 2),
-                Q(0, 0), F(st_g, 0), Q(0, 1), F(grad_flip, 0, 0, 0), F(st_y, 0), F(grad_flip, 0, 0, 1), Q(1, 0), F(st_p, 0),
-                F(grad_flip, 0, 1, 0), F(w_quant, "wo1", 0, wo_c[1], wo_s[1]), F(grad_flip, 0, 1, 1), F(st_s, 2), F(st_s, 3),
-                F(table_ln, (1, 0)), F(table_ln, (1, 1)), F(table_exp, (1, 0)), F(table_exp, (1, 1)), F(load_raw, "wk1", wk_t[1]),
-                F(st_g, 1), F(grad_quant, 0, 0), F(w_quant, "wo1", 1, wo_c[1], wo_s[1]), Q(1, 1), F(load_key, 4),
-                F(grad_quant, 0, 1), F(st_y, 1), F(st_p, 1),
+                F(x_flip, 0, 0, V), F(x_flip, 0, 1, V), F(x_diff, 0, 0), F(x_flip, 0, 2, V), F(x_diff, 0, 1), F(x_mix, 0, 0), F(x_flip, 0, 3, V), F(x_diff, 0, 2), F(x_mix, 0, 1),
+                F(table_exp, (0, 0)), F(table_ra, (0, 0)), F(table_exp, (0, 1)), F(table_ra, (0, 1)),
+                F(x_diff, 0, 3), Z(0, 0), F(x_mix, 0, 2), Z(0, 1), F(x_mix, 0, 3), F(st_s, 0),
+                F(w_il, "wo0", 0, V), F(w_il, "wo0", 1, V), Z(1, 0), F(w_quant, "wo0", 0, wo_c[0], wo_s[0]), Z(1, 1),  F(st_s, 1), F(w_quant, "wo0", 1, wo_c[0], wo_s[0]),
+                F(w_il, "wo1", 0, V), Z(2, 0), F(w_il, "wo1", 1, V), Z(2, 1), F(w_quant, "wo1", 0, wo_c[1], wo_s[1]), Q(0, 0), F(w_quant, "wo1", 1, wo_c[1], wo_s[1]), Q(0, 1), Z(3, 0), Z(3, 1),
+                F(load_val, 2), F(load_raw, "g1", grad_t[128:256]), F(load_gate, 2), F(grad_flip, 0, 0, 0), F(grad_flip, 0, 0, 1), F(st_y, 0),
+                F(grad_flip, 0, 1, 0), F(st_g, 0), F(grad_flip, 0, 1, 1), F(st_s, 2), F(st_s, 3), Q(1, 0), F(st_p, 0), Q(1, 1), F(grad_quant, 0, 0), F(st_g, 1), F(grad_quant, 0, 1),
+                F(table_ln, (1, 0)), F(table_ln, (1, 1)), F(table_exp, (1, 0)), F(table_ra, (1, 0)), F(table_exp, (1, 1)), F(table_ra, (1, 1)), F(load_raw, "wk0", wk_t[0]),
+                F(load_key, 4),
+                F(st_y, 1), F(st_p, 1),
             ]
             extra = {
-                0: [F(w_il, "wk0", 0, G), F(w_il, "wk0", 1, G), F(x_diff, 1, 0), F(table_ra, (1, 0)), F(table_ra, (1, 1))],
-                1: [F(w_quant, "wk0", 0, wk_c[0], wk_s[0]), F(load_raw, "g1", grad_t[128:256]), F(w_quant, "wk0", 1, wk_c[0], wk_s[0])],
-                2: [F(x_mix, 1, 0), F(grad_flip, 1, 0, 0), F(dkt_flip, 0), F(grad_flip, 1, 0, 1), F(dk_il, (0, 0), S), F(grad_flip, 1, 1, 0),
-                    F(x_quant, 1, 0), F(grad_flip, 1, 1, 1), F(dkt_quant, 0), F(w_il, "wk1", 0, S)],
-                3: [F(dkt_flip, 1), F(grad_quant, 1, 0), F(dk_quant, (0, 0)), F(grad_quant, 1, 1), F(dkt_flip, 2), F(w_quant, "wk1", 0, wk_c[1], wk_s[1]),
-                    F(w_il, "wk1", 1, S), F(dkt_quant, 1), F(dkt_quant, 2), F(dkt_flip, 3)],
-                4: [F(w_quant, "wk1", 1, wk_c[1], wk_s[1]), F(dk_il, (0, 1), S), X(0, 0, 0), X(0, 0, 1), F(dkt_quant, 3), F(flush), X(0, 1, 0), F(flush), X(0, 1, 1), F(flush),
-                    F(dk_quant, (0, 1)), F(flush), F(dkt_flip, 4)],
-                5: [X(0, 2, 0), X(0, 2, 1), F(flush), F(dkt_quant, 4), X(0, 3, 0), F(flush), F(dkt_flip, 5), X(0, 3, 1), F(x_diff, 1, 1), F(flush),
-                    F(flush), F(dk_il, (1, 0), S), F(dkt_quant, 5)],
-                6: [F(x_mix, 1, 1), F(dk_quant, (1, 0)), F(dkt_flip, 6), F(x_quant, 1, 1), F(dw, 0, 0, (S, S)), F(dkt_quant, 6), F(dw, 0, 1, (S, S)), X(1, 0, 0), X(1, 0, 1), F(dw, 0, 2, (S, S)), F(flush), F(flush)],
-                7: [F(dkt_flip, 7), F(dk_il, (1, 1), V), X(1, 1, 0), F(dk_quant, (1, 1)), X(1, 1, 1), F(dkt_quant, 7), F(flush), F(flush), X(1, 2, 0), X(1, 2, 1), X(1, 3, 0), X(1, 3, 1),
-                    F(dw, 0, 3, (S, S)), F(dw, 1, 0, (S, V)), F(dw, 1, 1, (S, V)), F(flush), F(dw, 1, 2, (S, V)), F(flush), F(dw, 1, 3, (S, V)),
-                     F(flush), F(flush)],
+                0: [F(x_flip, 0, 4, V), F(x_flip, 0, 5, V), F(x_diff, 0, 4), F(x_diff, 0, 5), F(x_mix, 0, 4), F(x_mix, 0, 5)],
+                1: [F(x_flip, 0, 6, V), F(x_flip, 0, 7, V), F(x_diff, 0, 6), F(x_diff, 0, 7), F(x_mix, 0, 6), F(x_mix, 0, 7), F(load_x, 1)],
+                2: [F(grad_flip, 1, 0, 0), F(grad_flip, 1, 0, 1), F(dkt_flip, 0), F(dk_il, (0, 0), S), F(grad_quant, 1, 0), F(grad_flip, 1, 1, 0), F(dkt_quant, 0),
+                    F(grad_flip, 1, 1, 1), F(load_raw, "wk1", wk_t[1]), F(w_il, "wk0", 0, S), F(w_il, "wk0", 1, S)],
+                3: [F(grad_quant, 1, 1), F(dkt_flip, 1), F(dk_quant, (0, 0)), F(x_flip, 1, 0, S), F(dkt_flip, 2), F(dkt_quant, 1), F(x_flip, 1, 1, S), F(w_quant, "wk0", 0, wk_c[0], wk_s[0]), F(w_quant, "wk0", 1, wk_c[0], wk_s[0]), F(w_il, "wk1", 0, S),
+                    F(x_diff, 1, 0), F(w_il, "wk1", 1, S), F(x_diff, 1, 1), F(dkt_quant, 2)],
+                4: [F(dkt_flip, 3), F(w_quant, "wk1", 0, wk_c[1], wk_s[1]), F(x_back, 0, 0), F(x_back, 0, 1), F(dk_il, (0, 1), S), F(w_quant, "wk1", 1, wk_c[1], wk_s[1]), F(dkt_quant, 3), F(x_back, 0, 2), F(x_back, 0, 3), F(x_flip, 1, 2, S), F(x_flip, 1, 3, S),
+                    X(0, 0), F(x_mix, 1, 0), X(0, 1), F(x_mix, 1, 1)],
+                5: [F(dk_quant, (0, 1)), X(0, 2), F(x_quant, 0, 0), F(x_diff, 1, 2), F(x_diff, 1, 3), X(0, 3), F(x_back, 0, 4), F(x_back, 0, 5), F(x_mix, 1, 2), X(0, 4), F(x_back, 0, 6), F(x_back, 0, 7),
+                    F(x_mix, 1, 3), X(0, 5), F(x_flip, 1, 4, S), F(x_flip, 1, 5, S), X(0, 6), F(x_quant, 0, 1), X(0, 7), F(dkt_flip, 4), F(dkt_flip, 5)],
+                6: [F(dk_il, (1, 0), S), F(x_back, 1, 0), F(x_back, 1, 1), F(x_diff, 1, 4), F(x_diff, 1, 5), F(x_back, 1, 2), F(x_back, 1, 3), F(x_flip, 1, 6, S), F(x_flip, 1, 7, S), F(x_mix, 1, 4), F(x_mix, 1, 5), F(dkt_quant, 4), F(dkt_quant, 5),
+                    F(x_quant, 1, 0), F(x_diff, 1, 6), F(x_diff, 1, 7), F(x_mix, 1, 6), F(x_mix, 1, 7), F(dk_quant, (1, 0)), F(dkt_flip, 6),
+                    F(x_back, 1, 4), F(x_back, 1, 5), F(x_back, 1, 6), F(x_back, 1, 7), F(dkt_quant, 6), F(x_quant, 1, 1)],
+                7: [F(dkt_flip, 7), F(dk_il, (1, 1), V), F(dw, 0, 0, (S, S)), F(dkt_quant, 7), F(dk_quant, (1, 1)), F(dw, 0, 1, (S, S)), F(dw, 0, 2, (S, S)), X(1, 0), X(1, 1), F(dw, 0, 3, (S, S)), X(1, 2), X(1, 3), F(dw, 1, 0, (S, S)), X(1, 4), X(1, 5), F(dw, 1, 1, (S, V)), X(1, 6), X(1, 7),
+                    F(dw, 1, 2, (S, V)), F(dw, 1, 3, (S, V))],
             }
             for i in range(8):
                 base = [D(i, 0), D(i, 1)]
@@ -486,7 +478,9 @@ def tile_rwkv_timemix_pa_v_kernel(
                         items.append(ex[0])
                         ex = ex[1:]
             run(items, 3)
+            V.tensor_tensor(out=tot[:, 0:8], in0=acc[:, 0:8], in1=acc[:, 8:16], op=ALU.add)
+            ps = bank("xp", (P, P))
+            PE.transpose(ps[:], tot[:], ident[:])
             row = stile("gate", [P, 2, 512], F32, 2)
-            S.copy(out=row[0:1, 0, :], in_=sums[0][0:1, :])
-            S.copy(out=row[0:1, 1, :], in_=sums[1][0:1, :])
-            nc.sync.dma_start(out=out_0.rearrange("(o i c) -> o i c", o=1, i=2), in_=row[0:1, :, :])
+            V.tensor_copy(out=row[:, 0, 0:128], in_=ps[:])
+            nc.sync.dma_start(out=out_0.rearrange("(r c) -> r c", c=P), in_=row[0:8, 0, 0:128])

from contextlib import ExitStack

import concourse.mybir as mybir
from concourse.masks import make_identity

F32 = mybir.dt.float32
BF16 = mybir.dt.bfloat16
U32 = mybir.dt.uint32
U8 = mybir.dt.uint8
E4M3 = mybir.dt.float8_e4m3fn_x4
E5M2 = mybir.dt.float8_e5m2_x4
ALU = mybir.AluOpType
ACT = mybir.ActivationFunctionType

B, T, C = 4, 256, 1024
EPS = 1e-8
FLOPS = 3 * 2 * (B * T) * C * C
BYTES = 4 * 2 * 1024 * 1024 + 3 * 4 * 1024 * 1024 + 3 * 2 * B * C + 3 * 2 * C + 4 * 1024 * 1024 + 4 * C

P = 128
ROW_A0, ROW_B0, ROW_W, ROW_U, ROW_MU = 0, 32, 64, 72, 80


def tile_rwkv_timemix_pa_v_kernel(
    tc, x, a0, b0, x_prev0, w, u, mu_r, mu_k, mu_v, W_r, W_k, W_v, W_out, gate, key, value, grad_out, out_0, out_1
):
    nc = tc.nc
    V, S, G, PE = nc.vector, nc.scalar, nc.gpsimd, nc.tensor

    def tokens(ap):
        return ap.rearrange("b (q j) c -> (b q) j c", j=4)

    x_t, grad_t, key_t, val_t, gate_t = tokens(x), tokens(grad_out), tokens(key), tokens(value), tokens(gate)
    wo_t = W_out.rearrange("(o p j) c -> o p j c", p=P, j=4)
    wk_t = W_k.rearrange("(o p j) c -> o p j c", p=P, j=4)

    with ExitStack() as ctx:
        const = ctx.enter_context(tc.tile_pool(name="const", bufs=1))
        st = ctx.enter_context(tc.tile_pool(name="st", bufs=2))
        psum = ctx.enter_context(tc.psum_pool(name="psum", bufs=2))

        def ctile(name, shape, dt):
            return const.tile(shape, dt, name=name, tag=name, bufs=1, align_bytes=64)

        def stile(tag, shape, dt, bufs):
            return st.tile(shape, dt, name=tag, tag=tag, bufs=bufs, align_bytes=64)

        banks = {"tp": 3, "dh": 3, "xp": 2}

        def bank(tag, shape=(P, 512), dt=F32):
            return psum.tile(list(shape), dt, name=tag, tag=tag, bufs=banks[tag])

        ident = ctile("ident", [P, P], F32)
        ident_b = ctile("ident_b", [P, P], BF16)
        steps = ctile("steps", [P, 256], F32)
        vt = ctile("vt", [P, P], BF16)
        vc = ctile("vc", [P, P], F32)
        eu = ctile("eu", [P, 8], F32)
        negw = ctile("negw", [P, 8], F32)
        beps = ctile("beps", [P, 8], F32)
        b0u = ctile("b0u", [P, 32], F32)
        b0m = ctile("b0m", [P, 32], F32)
        rb = ctile("rb", [P, 32], F32)
        c0 = ctile("c0", [P, 32], F32)
        nc1 = ctile("nc1", [P, 32], F32)
        dtab = ctile("dtab", [P, 8, 256], F32)
        acc = ctile("acc", [P, 16], F32)
        tot = ctile("tot", [P, P], F32)
        dummy = ctile("dummy", [P, 1], F32)

        wo_c = [ctile("wo_c%d" % o, [P, C], U32) for o in range(2)]
        wo_s = [ctile("wo_s%d" % o, [P, C], U8) for o in range(2)]
        wk_c = [ctile("wk_c%d" % o, [P, C], U32) for o in range(2)]
        wk_s = [ctile("wk_s%d" % o, [P, C], U8) for o in range(2)]
        gr_c = [ctile("gr_c%d" % g, [P, 2, 512], U32) for g in range(2)]
        gr_s = [ctile("gr_s%d" % g, [P, 2, 512], U8) for g in range(2)]
        xk_c = [ctile("xk_c%d" % g, [P, C], U32) for g in range(2)]
        xk_s = [ctile("xk_s%d" % g, [P, C], U8) for g in range(2)]
        dk_c = [[ctile("dk_c%d%d" % (g, h), [P, 512], U32) for h in range(2)] for g in range(2)]
        dk_s = [[ctile("dk_s%d%d" % (g, h), [P, 512], U8) for h in range(2)] for g in range(2)]
        dt_c, dt_s = {}, {}
        for h in range(2):
            dt_c[h] = ctile("dt_c%d" % h, [P, 512], U32)
            dt_s[h] = ctile("dt_s%d" % h, [P, 512], U8)

        V.memset(dummy[:], 0.0)
        V.memset(vt[:], 0.0)
        G.memset(tot[:], 0.0)
        make_identity(nc, ident_b[:])
        make_identity(nc, ident[:])
        G.iota(steps[:].rearrange("p (j q) -> p j q", j=4), pattern=[[1, 4], [4, 64]], base=1, channel_multiplier=0,
               allow_small_or_imprecise_dtypes=True)

        with tc.manual_schedule():
            S.activation(out=dummy[:], in_=dummy[:], func=ACT.Exp)
            nc.sync.dma_start(out=vt[ROW_W : ROW_W + 8, :], in_=w.rearrange("(r p) -> r p", p=P))
            nc.sync.dma_start(out=vt[ROW_U : ROW_U + 8, :], in_=u.rearrange("(r p) -> r p", p=P))
            nc.sync.dma_start(out=vt[ROW_B0 : ROW_B0 + 32, :], in_=b0.rearrange("b (r p) -> (b r) p", p=P))
            nc.sync.dma_start(out=vt[ROW_A0 : ROW_A0 + 32, :], in_=a0.rearrange("b (r p) -> (b r) p", p=P))
            nc.sync.dma_start(out=vt[ROW_MU : ROW_MU + 8, :], in_=mu_k.rearrange("(r p) -> r p", p=P))

            units = [(g, h, jp) for g in range(2) for h in range(2) for jp in range(2)]
            key_s, val_s, gate_s, raw_s, xm_s = {}, {}, {}, {}, {}

            def load_unit(store, tag, src, i, bufs):
                g, h, jp = units[i]
                t = stile(tag, [P, 2, 512], F32, bufs)
                nc.sync.dma_start(
                    out=t[:], in_=src[128 * g : 128 * g + 128, 2 * jp : 2 * jp + 2, 512 * h : 512 * h + 512]
                )
                store[i] = t

            def load_key(i):
                load_unit(key_s, "key", key_t, i, 4)

            def load_val(i):
                load_unit(val_s, "val", val_t, i, 3)

            def load_gate(i):
                load_unit(gate_s, "gate", gate_t, i, 2)

            def load_raw(name, src):
                t = stile("raw", [P, 4, C], BF16, 2)
                nc.sync.dma_start(out=t[:], in_=src)
                raw_s[name] = t

            def load_x(g):
                t = stile("xm", [P, 5, C], BF16, 1)
                nc.sync.dma_start(out=t[:, 1:5, :], in_=x_t[128 * g : 128 * g + 128])
                nc.sync.dma_start(out=t[1:64, 0, :], in_=x_t[128 * g : 128 * g + 63, 3, :])
                nc.sync.dma_start(out=t[65:128, 0, :], in_=x_t[128 * g + 64 : 128 * g + 127, 3, :])
                nc.sync.dma_start(out=t[0:1, 0, :], in_=x_prev0[2 * g : 2 * g + 1, :])
                nc.sync.dma_start(out=t[64:65, 0, :], in_=x_prev0[2 * g + 1 : 2 * g + 2, :])
                xm_s[g] = t

            load_x(0)
            load_key(0)
            load_key(1)

            vps = bank("tp", (P, P), BF16)
            PE.transpose(vps[:], vt[:], ident_b[:])
            V.tensor_copy(out=vc[:], in_=vps[:])
            S.activation(out=eu[:], in_=vc[:, ROW_U : ROW_U + 8], func=ACT.Exp, scale=-1.0)
            V.tensor_scalar(out=negw[:], in0=vc[:, ROW_W : ROW_W + 8], scalar1=-1.0, scalar2=None, op0=ALU.mult)
            V.tensor_scalar(out=b0m[:], in0=vc[:, ROW_B0 : ROW_B0 + 32], scalar1=1e-30, scalar2=None, op0=ALU.max)
            V.tensor_scalar(out=beps[:], in0=eu[:], scalar1=EPS, scalar2=None, op0=ALU.mult)

            def per_b(t):
                return t[:].rearrange("p (b r) -> p b r", b=4)

            def over_b(t):
                return t[:].unsqueeze(1).to_broadcast([P, 4, 8])

            V.tensor_tensor(out=per_b(b0u), in0=vc[:, ROW_B0 : ROW_B0 + 32].rearrange("p (b r) -> p b r", b=4),
                            in1=over_b(eu), op=ALU.mult)
            V.reciprocal(out=rb[:], in_=b0m[:])
            V.tensor_tensor(out=c0[:], in0=rb[:], in1=vc[:, ROW_A0 : ROW_A0 + 32], op=ALU.mult)
            V.scalar_tensor_tensor(out=per_b(nc1), in0=per_b(c0), scalar=-1.0, in1=over_b(beps), op0=ALU.mult, op1=ALU.mult)

            for r in range(8):
                S.activation(out=dtab[:, r, :], in_=steps[:], func=ACT.Exp, scale=negw[:, r : r + 1])

            tl, rt = {}, {}

            def table_ln(Q):
                g, h = Q
                t = stile("tl", [P, 4, 512], F32, 2)
                for r in range(4):
                    ct = 4 * h + r
                    dst = t[:, r, :].rearrange("p (j b q) -> p j b q", j=4, b=2)
                    for b2 in range(2):
                        col = 8 * (2 * g + b2) + ct
                        S.activation(out=dst[:, :, b2, :], in_=dtab[:, ct, :].rearrange("p (j q) -> p j q", j=4), func=ACT.Ln,
                                     scale=b0u[:, col : col + 1], bias=beps[:, ct : ct + 1])
                tl[Q] = t

            def table_exp(Q):
                t = stile("rt", [P, 4, 512], F32, 2)
                S.activation(out=t[:], in_=tl[Q][:], func=ACT.Exp, scale=-1.0)
                rt[Q] = t

            def table_ra(Q):
                g, h = Q
                for r in range(4):
                    ct = 4 * h + r
                    v = rt[Q][:, r, :].rearrange("p (j b q) -> p j b q", j=4, b=2)
                    for b2 in range(2):
                        col = 8 * (2 * g + b2) + ct
                        S.activation(out=v[:, :, b2, :], in_=v[:, :, b2, :], func=ACT.Identity, scale=nc1[:, col : col + 1],
                                     bias=c0[:, col : col + 1])

            dh_s, dkq = {}, {}

            def flip_table(tab, i, jj):
                g, h, jp = units[i]
                j = 2 * jp + jj
                tp = bank("tp")
                for r in range(4):
                    PE.transpose(tp[:, 128 * r : 128 * r + 128], tab[(g, h)][:, r, 128 * j : 128 * j + 128], ident[:])
                return tp

            tp_s = {}

            def pe_z(i, jj):
                tp_s[("z", i, jj)] = flip_table(tl, i, jj)

            def st_z(i, jj):
                V.tensor_tensor(out=key_s[i][:, jj, :], in0=key_s[i][:, jj, :], in1=tp_s[("z", i, jj)][:], op=ALU.subtract)

            def pe_q(i, jj):
                tp_s[("q", i, jj)] = flip_table(rt, i, jj)

            def st_s(i):
                S.activation(out=key_s[i][:], in_=key_s[i][:], func=ACT.Sigmoid)

            def st_q(i, jj):
                V.tensor_tensor(out=val_s[i][:, jj, :], in0=tp_s[("q", i, jj)][:], in1=val_s[i][:, jj, :], op=ALU.subtract)

            def st_y(i):
                V.tensor_tensor(out=val_s[i][:], in0=val_s[i][:], in1=gate_s[i][:], op=ALU.mult)

            def st_g(i):
                k = key_s[i]
                V.scalar_tensor_tensor(out=k[:], in0=k[:], scalar=1.0, in1=k[:], op0=ALU.subtract, op1=ALU.mult)

            def st_p(i):
                V.tensor_tensor(out=val_s[i][:], in0=val_s[i][:], in1=key_s[i][:], op=ALU.mult)

            def st_dh(i, jj):
                g, h, jp = units[i]
                j = 2 * jp + jj
                ps = bank("dh")
                for o in range(2):
                    PE.matmul_mx(ps[:], lhsT=gr_c[g][:, o, 128 * j : 128 * j + 128].bitcast(E5M2),
                                 lhsT_scale=gr_s[g][:, o, 128 * j : 128 * j + 128],
                                 rhs=wo_c[o][:, 512 * h : 512 * h + 512].bitcast(E4M3),
                                 rhs_scale=wo_s[o][:, 512 * h : 512 * h + 512], start=(o == 0), stop=(o == 1))
                dh_s[(i, jj)] = ps

            def st_d(i, jj):
                g, h, jp = units[i]
                if (g, h) not in dkq:
                    dkq[(g, h)] = stile("dkq", [P, 4, 512], BF16, 2)
                V.tensor_tensor(out=dkq[(g, h)][:, 2 * jp + jj, :], in0=dh_s[(i, jj)][:], in1=val_s[i][:, jj, :], op=ALU.mult)

            def words_view(til):
                return til.bitcast(F32).rearrange("p (j r e) -> p j r e", r=128, e=2)

            til_s = {}

            def flip_words(src, j0, col0, out_til):
                tp = bank("tp")
                for jj in range(2):
                    wds = src[:, j0 + jj, :].bitcast(F32)
                    for e in range(2):
                        k = 2 * jj + e
                        PE.transpose(tp[:, 128 * k : 128 * k + 128], wds[:, col0 + e : col0 + 256 : 2], ident[:])
                S.copy(out=words_view(out_til), in_=tp[:].rearrange("p (j e r) -> p j r e", j=2, e=2))

            def grad_flip(g, o, jp):
                if jp == 0:
                    til_s[("g", g, o)] = stile("til", [P, 2048], BF16, 2)
                flip_words(raw_s["g%d" % g], 2 * jp, 256 * o, til_s[("g", g, o)][:, 1024 * jp : 1024 * jp + 1024])

            def grad_quant(g, o):
                if True:
                    V.quantize_mx(out=gr_c[g][:, o, :].bitcast(E5M2), scales=gr_s[g][:, o, :], in_=til_s[("g", g, o)][:])

            def il_view(t):
                return t.rearrange("p (a i t) -> p a t i", i=4, t=4)

            def src_view(ap):
                return ap.rearrange("p t (a i) -> p a t i", i=4)

            il_s = {}

            def w_il(name, half, eng):
                t = stile("il", [P, 2048], BF16, 4)
                src = src_view(raw_s[name][:, :, 512 * half : 512 * half + 512])
                if eng is V:
                    V.tensor_copy(out=il_view(t[:]), in_=src)
                elif eng is G:
                    G.tensor_scalar(out=il_view(t[:]), in0=src, scalar1=1.0, scalar2=0.0, op0=ALU.mult, op1=ALU.add)
                else:
                    S.copy(out=il_view(t[:]), in_=src)
                il_s[(name, half)] = t

            def w_quant(name, half, codes, scales):
                sl = slice(512 * half, 512 * half + 512)
                V.quantize_mx(out=codes[:, sl].bitcast(E4M3), scales=scales[:, sl], in_=il_s[(name, half)][:])

            xt_s, df_s, xk_s2 = {}, {}, {}

            def x_flip(g, r, eng):
                ps = bank("xp", (P, 640), BF16)
                for s in range(5):
                    PE.transpose(ps[:, 128 * s : 128 * s + 128], xm_s[g][:, s, 128 * r : 128 * r + 128], ident_b[:])
                t = stile("xt", [P, 640], BF16, 3)
                if eng is V:
                    V.tensor_copy(out=t[:], in_=ps[:])
                else:
                    S.copy(out=t[:], in_=ps[:])
                xt_s[(g, r)] = t

            def x_diff(g, r):
                t = stile("df", [P, 512], F32, 14)
                V.tensor_tensor(out=t[:], in0=xt_s[(g, r)][:, 128:640], in1=xt_s[(g, r)][:, 0:512], op=ALU.subtract)
                df_s[(g, r)] = t

            def x_mix(g, r):
                t = stile("xk", [P, 512], BF16, 8)
                V.scalar_tensor_tensor(out=t[:], in0=df_s[(g, r)][:], scalar=vc[:, ROW_MU + r : ROW_MU + r + 1],
                                       in1=xt_s[(g, r)][:, 0:512], op0=ALU.mult, op1=ALU.add)
                xk_s2[(g, r)] = t

            def x_back(g, r, eng=None):
                ps = bank("xp", (P, 512), BF16)
                for j in range(4):
                    PE.transpose(ps[:, 128 * j : 128 * j + 128], xk_s2[(g, r)][:, 128 * j : 128 * j + 128], ident_b[:])
                if r % 4 == 0:
                    il_s[("x", g, r // 4)] = stile("il", [P, 2048], BF16, 4)
                k = r % 4
                dst = il_s[("x", g, r // 4)][:, 512 * k : 512 * k + 512].rearrange("p (c t) -> p c t", t=4)
                S.copy(out=dst, in_=ps[:].rearrange("p (t c) -> p c t", t=4))

            def x_quant(g, nh):
                sl = slice(512 * nh, 512 * nh + 512)
                V.quantize_mx(out=xk_c[g][:, sl].bitcast(E4M3), scales=xk_s[g][:, sl], in_=il_s[("x", g, nh)][:])

            def dkt_flip(i):
                g, h, jp = units[i]
                t = stile("til", [P, 2048], BF16, 2)
                flip_words(dkq[(g, h)], 2 * jp, 0, t[:, 0:1024])
                til_s[("d", i)] = t

            def dkt_quant(i):
                g, h, jp = units[i]
                sl = slice(256 * jp, 256 * jp + 256)
                V.quantize_mx(out=dt_c[h][:, sl].bitcast(E5M2), scales=dt_s[h][:, sl], in_=til_s[("d", i)][:, 0:1024])

            def dk_il(Q, eng):
                t = stile("il", [P, 2048], BF16, 4)
                if eng is V:
                    V.tensor_copy(out=il_view(t[:]), in_=src_view(dkq[Q][:]))
                else:
                    S.copy(out=il_view(t[:]), in_=src_view(dkq[Q][:]))
                il_s[("d", Q)] = t

            def dk_quant(Q):
                g, h = Q
                V.quantize_mx(out=dk_c[g][h][:].bitcast(E5M2), scales=dk_s[g][h][:], in_=il_s[("d", Q)][:])

            dx_s = {}

            def pe_dx(g, r):
                ps = bank("dh")
                for h in range(2):
                    PE.matmul_mx(ps[:], lhsT=wk_c[h][:, 128 * r : 128 * r + 128].bitcast(E4M3),
                                 lhsT_scale=wk_s[h][:, 128 * r : 128 * r + 128],
                                 rhs=dt_c[h][:].bitcast(E5M2), rhs_scale=dt_s[h][:], start=(h == 0), stop=(h == 1))
                dx_s[(g, r)] = ps

            def st_dx(g, r):
                prod = stile("prod", [P, 512], F32, 1)
                V.scalar_tensor_tensor(out=prod[:], in0=dx_s[(g, r)][:], scalar=1.0, in1=df_s[(g, r)][:], op0=ALU.mult, op1=ALU.mult,
                                       accum_out=acc[:, 8 * g + r : 8 * g + r + 1])

            def dw(h, co, engs, tag="tp"):
                t = stile("key", [P, 2, 512], F32, 4)
                for ci in range(2):
                    ps = bank(tag)
                    for g in range(2):
                        PE.matmul_mx(ps[:], lhsT=dk_c[g][h][:, 128 * co : 128 * co + 128].bitcast(E5M2),
                                     lhsT_scale=dk_s[g][h][:, 128 * co : 128 * co + 128],
                                     rhs=xk_c[g][:, 512 * ci : 512 * ci + 512].bitcast(E4M3),
                                     rhs_scale=xk_s[g][:, 512 * ci : 512 * ci + 512], start=(g == 0), stop=(g == 1))
                    if engs[ci] is V:
                        V.tensor_copy(out=t[:, ci, :], in_=ps[:])
                    else:
                        S.copy(out=t[:, ci, :], in_=ps[:])
                r0 = 512 * h + 128 * co
                nc.sync.dma_start(out=out_1[r0 : r0 + 128, :].rearrange("p (i c) -> p i c", i=2), in_=t[:])

            made = set()

            def F(f, *a):
                def go():
                    f(*a)
                    made.add((f,) + tuple(v for v in a[:2] if isinstance(v, (int, str, tuple))))

                return (None, go, ())

            def Z(i, jj):
                return (lambda: pe_z(i, jj), lambda: st_z(i, jj), ())

            def Q(i, jj):
                return (lambda: pe_q(i, jj), lambda: st_q(i, jj), ((table_ra, units[i][:2]),))

            def D(i, jj):
                return (lambda: st_dh(i, jj), lambda: st_d(i, jj), ((grad_quant, units[i][0], 1), (w_quant, "wo1", 1)))

            def X(g, r):
                return (lambda: pe_dx(g, r), lambda: st_dx(g, r), ((dkt_quant, 4 * g + 2), (dkt_quant, 4 * g + 3), (w_quant, "wk1", 1)))

            def run(items, ahead):
                front = 0
                for k in range(-ahead, len(items)):
                    while front < min(k + ahead + 1, len(items)) and all(t in made for t in items[front][2]):
                        if items[front][0] is not None:
                            items[front][0]()
                        front += 1
                    if k >= 0:
                        assert front > k
                        items[k][1]()

            load_raw("wo0", wo_t[0])
            load_key(2)
            load_raw("wo1", wo_t[1])
            load_val(0)
            load_gate(0)
            load_raw("g0", grad_t[0:128])
            load_key(3)
            load_val(1)
            load_gate(1)
            table_ln((0, 0))
            table_ln((0, 1))

            items = [
                F(x_flip, 0, 0, V), F(x_flip, 0, 1, V), F(x_diff, 0, 0), F(x_flip, 0, 2, V), F(x_diff, 0, 1), F(x_mix, 0, 0), F(x_flip, 0, 3, V), F(x_diff, 0, 2), F(x_mix, 0, 1),
                F(table_exp, (0, 0)), F(table_ra, (0, 0)), F(table_exp, (0, 1)), F(table_ra, (0, 1)),
                F(x_diff, 0, 3), Z(0, 0), F(x_mix, 0, 2), Z(0, 1), F(x_mix, 0, 3), F(st_s, 0),
                F(w_il, "wo0", 0, V), F(w_il, "wo0", 1, V), Z(1, 0), F(w_quant, "wo0", 0, wo_c[0], wo_s[0]), Z(1, 1),  F(st_s, 1), F(w_quant, "wo0", 1, wo_c[0], wo_s[0]),
                F(w_il, "wo1", 0, V), Z(2, 0), F(w_il, "wo1", 1, V), Z(2, 1), F(w_quant, "wo1", 0, wo_c[1], wo_s[1]), Q(0, 0), F(w_quant, "wo1", 1, wo_c[1], wo_s[1]), Q(0, 1), Z(3, 0), Z(3, 1),
                F(load_val, 2), F(load_raw, "g1", grad_t[128:256]), F(load_gate, 2), F(grad_flip, 0, 0, 0), F(grad_flip, 0, 0, 1), F(st_y, 0),
                F(grad_flip, 0, 1, 0), F(st_g, 0), F(grad_flip, 0, 1, 1), F(st_s, 2), F(st_s, 3), Q(1, 0), F(st_p, 0), Q(1, 1), F(grad_quant, 0, 0), F(st_g, 1), F(grad_quant, 0, 1),
                F(table_ln, (1, 0)), F(table_ln, (1, 1)), F(table_exp, (1, 0)), F(table_ra, (1, 0)), F(table_exp, (1, 1)), F(table_ra, (1, 1)), F(load_raw, "wk0", wk_t[0]),
                F(load_key, 4),
                F(st_y, 1), F(st_p, 1),
            ]
            extra = {
                0: [F(x_flip, 0, 4, V), F(x_flip, 0, 5, V), F(x_diff, 0, 4), F(x_diff, 0, 5), F(x_mix, 0, 4), F(x_mix, 0, 5)],
                1: [F(x_flip, 0, 6, V), F(x_flip, 0, 7, V), F(x_diff, 0, 6), F(x_diff, 0, 7), F(x_mix, 0, 6), F(x_mix, 0, 7), F(load_x, 1)],
                2: [F(grad_flip, 1, 0, 0), F(grad_flip, 1, 0, 1), F(dkt_flip, 0), F(dk_il, (0, 0), S), F(grad_quant, 1, 0), F(grad_flip, 1, 1, 0), F(dkt_quant, 0),
                    F(grad_flip, 1, 1, 1), F(load_raw, "wk1", wk_t[1]), F(w_il, "wk0", 0, S), F(w_il, "wk0", 1, S)],
                3: [F(grad_quant, 1, 1), F(dkt_flip, 1), F(dk_quant, (0, 0)), F(x_flip, 1, 0, S), F(dkt_flip, 2), F(dkt_quant, 1), F(x_flip, 1, 1, S), F(w_quant, "wk0", 0, wk_c[0], wk_s[0]), F(w_quant, "wk0", 1, wk_c[0], wk_s[0]), F(w_il, "wk1", 0, S),
                    F(x_diff, 1, 0), F(w_il, "wk1", 1, S), F(x_diff, 1, 1), F(dkt_quant, 2)],
                4: [F(dkt_flip, 3), F(w_quant, "wk1", 0, wk_c[1], wk_s[1]), F(x_back, 0, 0), F(x_back, 0, 1), F(dk_il, (0, 1), S), F(w_quant, "wk1", 1, wk_c[1], wk_s[1]), F(dkt_quant, 3), F(x_back, 0, 2), F(x_back, 0, 3), F(x_flip, 1, 2, S), F(x_flip, 1, 3, S),
                    X(0, 0), F(x_mix, 1, 0), X(0, 1), F(x_mix, 1, 1)],
                5: [F(dk_quant, (0, 1)), X(0, 2), F(x_quant, 0, 0), F(x_diff, 1, 2), F(x_diff, 1, 3), X(0, 3), F(x_back, 0, 4), F(x_back, 0, 5), F(x_mix, 1, 2), X(0, 4), F(x_back, 0, 6), F(x_back, 0, 7),
                    F(x_mix, 1, 3), X(0, 5), F(x_flip, 1, 4, S), F(x_flip, 1, 5, S), X(0, 6), F(x_quant, 0, 1), X(0, 7), F(dkt_flip, 4), F(dkt_flip, 5)],
                6: [F(dk_il, (1, 0), S), F(x_back, 1, 0), F(x_back, 1, 1), F(x_diff, 1, 4), F(x_diff, 1, 5), F(x_back, 1, 2), F(x_back, 1, 3), F(x_flip, 1, 6, S), F(x_flip, 1, 7, S), F(x_mix, 1, 4), F(x_mix, 1, 5), F(dkt_quant, 4), F(dkt_quant, 5),
                    F(x_quant, 1, 0), F(x_diff, 1, 6), F(x_diff, 1, 7), F(x_mix, 1, 6), F(x_mix, 1, 7), F(dk_quant, (1, 0)), F(dkt_flip, 6),
                    F(x_back, 1, 4), F(x_back, 1, 5), F(x_back, 1, 6), F(x_back, 1, 7), F(dkt_quant, 6), F(x_quant, 1, 1)],
                7: [F(dkt_flip, 7), F(dk_il, (1, 1), V), F(dw, 0, 0, (S, S)), F(dkt_quant, 7), F(dk_quant, (1, 1)), F(dw, 0, 1, (S, S)), F(dw, 0, 2, (S, S)), X(1, 0), X(1, 1), F(dw, 0, 3, (S, S)), X(1, 2), X(1, 3), F(dw, 1, 0, (S, S)), X(1, 4), X(1, 5), F(dw, 1, 1, (S, V)), X(1, 6), X(1, 7),
                    F(dw, 1, 2, (S, V)), F(dw, 1, 3, (S, V))],
            }
            for i in range(8):
                base = [D(i, 0), D(i, 1)]
                if 1 <= i < 7:
                    base = [Q(i + 1, 0), D(i, 0), Q(i + 1, 1), D(i, 1), F(st_g, i + 1), F(st_y, i + 1), F(st_p, i + 1)]
                if i == 0:
                    base = [D(0, 0), D(0, 1)]
                if 1 <= i <= 4:
                    base += [Z(i + 3, 0), Z(i + 3, 1), F(st_s, i + 3)]
                if i + 5 < 8:
                    base.append(F(load_key, i + 5))
                if i + 3 < 8:
                    base += [F(load_gate, i + 3), F(load_val, i + 3)]
                ex = extra[i]
                lead = 4 if 1 <= i < 7 else len(base)
                items += base[:lead]
                rest = base[lead:]
                while rest or ex:
                    if rest:
                        items.append(rest[0])
                        rest = rest[1:]
                    if ex:
                        items.append(ex[0])
                        ex = ex[1:]
            run(items, 3)
            V.tensor_tensor(out=tot[:, 0:8], in0=acc[:, 0:8], in1=acc[:, 8:16], op=ALU.add)
            ps = bank("xp", (P, P))
            PE.transpose(ps[:], tot[:], ident[:])
            row = stile("gate", [P, 2, 512], F32, 2)
            V.tensor_copy(out=row[:, 0, 0:128], in_=ps[:])
            nc.sync.dma_start(out=out_0.rearrange("(r c) -> r c", c=P), in_=row[0:8, 0, 0:128])
